import numpy as np
import ml_dtypes


def mxq(x, axis, fmt="e4m3"):
    dtype, down = {"e4m3": (ml_dtypes.float8_e4m3fn, 7), "e5m2": (ml_dtypes.float8_e5m2, 14)}[fmt]
    v = np.moveaxis(np.asarray(x, np.float32).astype(ml_dtypes.bfloat16).astype(np.float64), axis, -1)
    blocks = v.reshape(v.shape[:-1] + (-1, 32))
    amax = np.abs(blocks).max(-1, keepdims=True)
    byte = np.maximum(np.where(amax > 0, np.frexp(amax)[1] - 1 + 127, 0) - down, 1)
    scale = np.exp2(byte - 127.0)
    codes = (blocks / scale).astype(np.float32).astype(dtype).astype(np.float64)
    return np.moveaxis((codes * scale).reshape(v.shape), -1, axis)


WIDE = False


def mx_kscale(k):
    if not WIDE:
        return np.ones(k)
    levels = np.array([10, -10, 5, -5, 0])
    a = np.random.permutation(np.resize(levels, k // 512 * 4)).reshape(k // 512, 4)
    idx = np.arange(k)
    return np.exp2(a[idx // 512, idx % 128 // 32])


BF16 = ml_dtypes.bfloat16


def bf(x):
    return np.asarray(x, np.float32).astype(BF16)


def f64(x):
    return np.asarray(x).astype(np.float64)


B, N, D, DO, H, HID = 64, 128, 512, 256, 8, 2048


def setup_inputs():
    s, t = mx_kscale(D), mx_kscale(D)
    adj = np.random.uniform(size=(N, N))
    adj = adj / adj.sum(-1, keepdims=True)
    return {
        "h_norm": bf(np.random.standard_normal((B, N, D)) * s),
        "o_attn": bf(np.random.standard_normal((B, N, D)) * 0.25 * t),
        "a_gcn": bf(adj + np.random.standard_normal((N, N)) * 0.5 / np.sqrt(N)),
        "w_proj": bf(np.random.standard_normal((D, DO)) * 2.0 / np.sqrt(D) / t[:, None]),
        "b_proj": bf(np.random.standard_normal(DO) * 0.1),
        "gcn_w": bf(np.random.standard_normal((D, DO)) / np.sqrt(D) / s[:, None]),
        "gcn_m": bf(1.0 + 0.1 * np.random.standard_normal(DO)),
    }


def reference(h_norm, o_attn, a_gcn, w_proj, b_proj, gcn_w, gcn_m):
    o = (mxq(f64(o_attn), 2, "e4m3") @ mxq(f64(w_proj), 0, "e4m3")) + f64(b_proj)
    agg = f64(a_gcn) @ f64(h_norm)
    g = (mxq(agg, 2, "e4m3") @ mxq(f64(gcn_w), 0, "e4m3")) * f64(gcn_m)
    return o + g

@@ -1,0 +1,198 @@
+from contextlib import ExitStack
+
+import concourse.masks as masks
+import concourse.mybir as mybir
+
+F32 = mybir.dt.float32
+BF16 = mybir.dt.bfloat16
+U32 = mybir.dt.uint32
+U8 = mybir.dt.uint8
+FP8X4 = mybir.dt.float8_e4m3fn_x4
+MULT = mybir.AluOpType.mult
+ADD = mybir.AluOpType.add
+
+P = 128
+B, N, D, DO = 64, 128, 512, 256
+T = 4
+NBLK = B // T
+LEAD = 8
+FLOPS = 2 * 2 * B * N * D * DO + 2 * B * N * N * D
+
+
+def tile_gatblock_pa_t_kernel(tc, h_norm, o_attn, a_gcn, w_proj, b_proj, gcn_w, gcn_m, out):
+    nc = tc.nc
+    o_blk = o_attn.flatten_outer_dims().rearrange("(k p j) d -> k p (j d)", p=P, j=T)
+    out_blk = out.flatten_outer_dims().rearrange("(k p j) c -> k p (j c)", p=P, j=T)
+    h_blk = h_norm.rearrange("(k b) n d -> k n b d", b=T)
+
+    with ExitStack() as ctx:
+        consts = ctx.enter_context(tc.tile_pool(name="consts", bufs=1))
+        inputs = ctx.enter_context(tc.tile_pool(name="inputs", bufs=LEAD + 2))
+        work = ctx.enter_context(tc.tile_pool(name="work", bufs=2))
+        outs = ctx.enter_context(tc.tile_pool(name="outs", bufs=3))
+        ps_a = ctx.enter_context(tc.psum_pool(name="ps_a", bufs=4))
+        ps_m = ctx.enter_context(tc.psum_pool(name="ps_m", bufs=1))
+        ctx.enter_context(tc.manual_schedule())
+
+        o_tiles, h_tiles, go_tiles, gg_tiles = {}, {}, {}, {}
+        oc_tiles, os_tiles, gc_tiles, gs_tiles = {}, {}, {}, {}
+        mg_tiles, mo_tiles, res_tiles = {}, {}, {}
+
+        def load(k):
+            o_sb = inputs.tile([P, T * D], BF16)
+            nc.sync.dma_start(out=o_sb[:], in_=o_blk[k])
+            h_sb = inputs.tile([P, T, D], BF16)
+            nc.sync.dma_start(out=h_sb[:], in_=h_blk[k])
+            o_tiles[k] = o_sb
+            h_tiles[k] = h_sb
+
+        a_sb = consts.tile([P, P], BF16)
+        nc.sync.dma_start(out=a_sb[:], in_=a_gcn)
+        w_raw = consts.tile([P, 2, 4, DO], BF16)
+        nc.scalar.dma_start(
+            out=w_raw[:, 0, :, :].rearrange("p (u e) c -> p u (e c)", u=2),
+            in_=w_proj.rearrange("(u p e) c -> p u (e c)", u=2, e=2),
+        )
+        nc.scalar.dma_start(out=w_raw[:, 1, :, :], in_=gcn_w.rearrange("(t p) c -> p t c", p=P))
+        vec_rows = consts.tile([P, 2 * DO], BF16)
+        nc.vector.memset(vec_rows[:], 0.0)
+        nc.scalar.dma_start(out=vec_rows[0:1, 0:DO], in_=gcn_m.rearrange("(o c) -> o c", o=1))
+        nc.scalar.dma_start(out=vec_rows[0:1, DO : 2 * DO], in_=b_proj.rearrange("(o c) -> o c", o=1))
+        for k in range(LEAD):
+            load(k)
+
+        ident = consts.tile([P, P], F32)
+        masks.make_identity(nc, ident[:])
+        ones = consts.tile([P, P], BF16)
+        nc.vector.memset(ones[:], 1.0)
+        ident_bf = consts.tile([P, P], BF16)
+        nc.vector.tensor_copy(out=ident_bf[:], in_=ident[:])
+        at_ps = ps_a.tile([P, P], BF16, tag="a")
+        nc.tensor.transpose(at_ps[:], a_sb[:], ident_bf[:])
+        a_t = consts.tile([P, P], BF16)
+        nc.vector.tensor_copy(out=a_t[:], in_=at_ps[:])
+
+        w_grp = consts.tile([P, 2, DO, 4], BF16, align_bytes=64)
+        for w in range(2):
+            nc.vector.tensor_copy(out=w_grp[:, w, :, :], in_=w_raw[:, w, :, :].rearrange("p t c -> p c t"))
+        w_codes = consts.tile([P, 2 * DO], U32, align_bytes=64)
+        w_scales = consts.tile([P, 2 * DO], U8, align_bytes=64)
+        nc.vector.quantize_mx(
+            out=w_codes[:].bitcast(FP8X4), scales=w_scales[:], in_=w_grp[:].rearrange("p w c t -> p (w c t)")
+        )
+        m_bc = consts.tile([P, 2, DO], F32)
+        b_bc = consts.tile([P, 2, DO], F32)
+
+        def spread_vectors():
+            vec_ps = ps_a.tile([P, 2 * DO], F32, tag="a")
+            nc.tensor.matmul(vec_ps[:], lhsT=ones[:], rhs=vec_rows[:], start=True, stop=True)
+            for r in range(2):
+                nc.vector.tensor_copy(out=m_bc[:, r, :], in_=vec_ps[:, 0:DO])
+                nc.vector.tensor_copy(out=b_bc[:, r, :], in_=vec_ps[:, DO : 2 * DO])
+
+        def transposes(i):
+            o_words = o_tiles[i][:].bitcast(F32)
+            go = work.tile([P, T * P * 4], BF16, align_bytes=64)
+            go_tiles[i] = go
+            go_words = go[:].bitcast(F32).rearrange("p (j r u) -> p j r u", j=T, u=2)
+            for half in range(2):
+                xt = ps_a.tile([P, 2, 2, P], F32, tag="a")
+                for jj in range(2):
+                    for u in range(2):
+                        c0 = 256 * (2 * half + jj) + P * u
+                        nc.tensor.transpose(xt[:, jj, u, :], o_words[:, c0 : c0 + P], ident[:])
+                nc.scalar.copy(
+                    out=go_words[:, 2 * half : 2 * half + 2, :, :], in_=xt[:].rearrange("p j u r -> p j r u")
+                )
+
+        def mix(i, b):
+            if b == 0:
+                gg = work.tile([P, T, P, 4], BF16, align_bytes=64)
+                gg_tiles[i] = gg
+            ag = ps_a.tile([P, 4, P], F32, tag="a")
+            for t in range(4):
+                nc.tensor.matmul(
+                    ag[:, t, :], lhsT=h_tiles[i][:, b, P * t : P * t + P], rhs=a_t[:], start=True, stop=True
+                )
+            nc.scalar.copy(
+                out=gg_tiles[i][:, :, 32 * b : 32 * b + 32, :], in_=ag[:].rearrange("p t (r j) -> p j r t", j=T)
+            )
+
+        def quantise_o(i):
+            oc = work.tile([P, T * P], U32, align_bytes=64)
+            osc = work.tile([P, T * P], U8, align_bytes=64)
+            nc.vector.quantize_mx(out=oc[:].bitcast(FP8X4), scales=osc[:], in_=go_tiles[i][:])
+            oc_tiles[i] = oc
+            os_tiles[i] = osc
+
+        def quantise_g(i):
+            gc = work.tile([P, T * P], U32, align_bytes=64)
+            gsc = work.tile([P, T * P], U8, align_bytes=64)
+            nc.vector.quantize_mx(
+                out=gc[:].bitcast(FP8X4), scales=gsc[:], in_=gg_tiles[i][:].rearrange("p j r t -> p (j r t)")
+            )
+            gc_tiles[i] = gc
+            gs_tiles[i] = gsc
+
+        def mx_passes(i):
+            for which, codes, scales, keep in (
+                (1, gc_tiles[i], gs_tiles[i], mg_tiles),
+                (0, oc_tiles[i], os_tiles[i], mo_tiles),
+            ):
+                for half in range(2):
+                    acc = ps_m.tile([P, 2, DO], F32, tag="m%d%d" % (which, half))
+                    keep[(i, half)] = acc
+                    for jj in range(2):
+                        c0 = P * (2 * half + jj)
+                        nc.tensor.matmul_mx(
+                            out=acc[:, jj, :],
+                            lhsT=codes[:, c0 : c0 + P].bitcast(FP8X4),
+                            lhsT_scale=scales[:, c0 : c0 + P],
+                            rhs=w_codes[:, DO * which : DO * which + DO].bitcast(FP8X4),
+                            rhs_scale=w_scales[:, DO * which : DO * which + DO],
+                            start=True,
+                            stop=True,
+                        )
+
+        def scale_g(i, half):
+            if half == 0:
+                res = outs.tile([P, T, DO], F32)
+                res_tiles[i] = res
+            part = res_tiles[i][:, 2 * half : 2 * half + 2, :]
+            nc.vector.tensor_tensor(out=part, in0=mg_tiles[(i, half)][:], in1=m_bc[:], op=MULT)
+
+        def add_o(i, half):
+            part = res_tiles[i][:, 2 * half : 2 * half + 2, :]
+            nc.vector.tensor_tensor(out=part, in0=mo_tiles[(i, half)][:], in1=part, op=ADD)
+            nc.gpsimd.tensor_tensor(out=part, in0=part, in1=b_bc[:], op=ADD)
+
+        def store(i):
+            nc.sync.dma_start(out=out_blk[i], in_=res_tiles[i][:].rearrange("p j c -> p (j c)"))
+
+        def live(i):
+            return 0 <= i < NBLK
+
+        for i in range(-2, NBLK + 1):
+            if i == 0:
+                spread_vectors()
+            if live(i):
+                quantise_g(i)
+            if live(i - 1):
+                add_o(i - 1, 1)
+                store(i - 1)
+            if live(i):
+                mx_passes(i)
+            if live(i + 1):
+                mix(i + 1, 2)
+                mix(i + 1, 3)
+                quantise_o(i + 1)
+            if live(i):
+                scale_g(i, 0)
+                scale_g(i, 1)
+                add_o(i, 0)
+            if live(i + 2):
+                transposes(i + 2)
+                mix(i + 2, 0)
+                mix(i + 2, 1)
+            if live(i + 2 + LEAD):
+                load(i + 2 + LEAD)

@@ -16,6 +16,7 @@ B, N, D, DO = 64, 128, 512, 256
 T = 4
 NBLK = B // T
 LEAD = 8
+AHEAD = 3
 FLOPS = 2 * 2 * B * N * D * DO + 2 * B * N * N * D
 
 
@@ -27,39 +28,43 @@ def tile_gatblock_pa_t_kernel(tc, h_norm, o_attn, a_gcn, w_proj, b_proj, gcn_w, 
 
     with ExitStack() as ctx:
         consts = ctx.enter_context(tc.tile_pool(name="consts", bufs=1))
-        inputs = ctx.enter_context(tc.tile_pool(name="inputs", bufs=LEAD + 2))
-        work = ctx.enter_context(tc.tile_pool(name="work", bufs=2))
-        outs = ctx.enter_context(tc.tile_pool(name="outs", bufs=3))
+        inputs = ctx.enter_context(tc.tile_pool(name="inputs", bufs=LEAD + 3))
+        work = ctx.enter_context(tc.tile_pool(name="work", bufs=3))
+        outs = ctx.enter_context(tc.tile_pool(name="outs", bufs=8))
         ps_a = ctx.enter_context(tc.psum_pool(name="ps_a", bufs=4))
         ps_m = ctx.enter_context(tc.psum_pool(name="ps_m", bufs=1))
         ctx.enter_context(tc.manual_schedule())
 
-        o_tiles, h_tiles, go_tiles, gg_tiles = {}, {}, {}, {}
-        oc_tiles, os_tiles, gc_tiles, gs_tiles = {}, {}, {}, {}
-        mg_tiles, mo_tiles, res_tiles = {}, {}, {}
+        o_tiles, h_tiles, grp_tiles, code_tiles, scale_tiles = {}, {}, {}, {}, {}
+        acc_tiles, res_tiles = {}, {}
 
-        def load(k):
+        def load(k, pieces):
             o_sb = inputs.tile([P, T * D], BF16)
-            nc.sync.dma_start(out=o_sb[:], in_=o_blk[k])
             h_sb = inputs.tile([P, T, D], BF16)
-            nc.sync.dma_start(out=h_sb[:], in_=h_blk[k])
             o_tiles[k] = o_sb
             h_tiles[k] = h_sb
+            wo = T * D // pieces
+            for q in range(pieces):
+                nc.sync.dma_start(out=o_sb[:, q * wo : (q + 1) * wo], in_=o_blk[k][:, q * wo : (q + 1) * wo])
+            wh = T // pieces
+            for q in range(pieces):
+                nc.sync.dma_start(out=h_sb[:, q * wh : (q + 1) * wh, :], in_=h_blk[k][:, q * wh : (q + 1) * wh, :])
 
         a_sb = consts.tile([P, P], BF16)
         nc.sync.dma_start(out=a_sb[:], in_=a_gcn)
+        vec_rows = consts.tile([P, 2 * DO], BF16)
+        nc.vector.memset(vec_rows[:], 0.0)
+        nc.sync.dma_start(out=vec_rows[0:1, 0:DO], in_=gcn_m.rearrange("(o c) -> o c", o=1))
+        nc.sync.dma_start(out=vec_rows[0:1, DO : 2 * DO], in_=b_proj.rearrange("(o c) -> o c", o=1))
         w_raw = consts.tile([P, 2, 4, DO], BF16)
-        nc.scalar.dma_start(
+        nc.sync.dma_start(out=w_raw[:, 1, :, :], in_=gcn_w.rearrange("(t p) c -> p t c", p=P))
+        nc.sync.dma_start(
             out=w_raw[:, 0, :, :].rearrange("p (u e) c -> p u (e c)", u=2),
             in_=w_proj.rearrange("(u p e) c -> p u (e c)", u=2, e=2),
         )
-        nc.scalar.dma_start(out=w_raw[:, 1, :, :], in_=gcn_w.rearrange("(t p) c -> p t c", p=P))
-        vec_rows = consts.tile([P, 2 * DO], BF16)
-        nc.vector.memset(vec_rows[:], 0.0)
-        nc.scalar.dma_start(out=vec_rows[0:1, 0:DO], in_=gcn_m.rearrange("(o c) -> o c", o=1))
-        nc.scalar.dma_start(out=vec_rows[0:1, DO : 2 * DO], in_=b_proj.rearrange("(o c) -> o c", o=1))
-        for k in range(LEAD):
-            load(k)
+        load(0, 2)
+        for k in range(1, LEAD):
+            load(k, 1)
 
         ident = consts.tile([P, P], F32)
         masks.make_identity(nc, ident[:])
@@ -72,29 +77,28 @@ def tile_gatblock_pa_t_kernel(tc, h_norm, o_attn, a_gcn, w_proj, b_proj, gcn_w, 
         a_t = consts.tile([P, P], BF16)
         nc.vector.tensor_copy(out=a_t[:], in_=at_ps[:])
 
+        m_bc = consts.tile([P, 2, DO], F32)
+        b_bc = consts.tile([P, 2, DO], F32)
+        vec_ps = ps_a.tile([P, 2 * DO], F32, tag="a")
+        nc.tensor.matmul(vec_ps[:], lhsT=ones[:], rhs=vec_rows[:], start=True, stop=True)
+        for r in range(2):
+            nc.vector.tensor_copy(out=m_bc[:, r, :], in_=vec_ps[:, 0:DO])
+            nc.vector.tensor_copy(out=b_bc[:, r, :], in_=vec_ps[:, DO : 2 * DO])
+
         w_grp = consts.tile([P, 2, DO, 4], BF16, align_bytes=64)
-        for w in range(2):
-            nc.vector.tensor_copy(out=w_grp[:, w, :, :], in_=w_raw[:, w, :, :].rearrange("p t c -> p c t"))
         w_codes = consts.tile([P, 2 * DO], U32, align_bytes=64)
         w_scales = consts.tile([P, 2 * DO], U8, align_bytes=64)
+        for w in (1, 0):
+            nc.vector.tensor_copy(out=w_grp[:, w, :, :], in_=w_raw[:, w, :, :].rearrange("p t c -> p c t"))
         nc.vector.quantize_mx(
             out=w_codes[:].bitcast(FP8X4), scales=w_scales[:], in_=w_grp[:].rearrange("p w c t -> p (w c t)")
         )
-        m_bc = consts.tile([P, 2, DO], F32)
-        b_bc = consts.tile([P, 2, DO], F32)
-
-        def spread_vectors():
-            vec_ps = ps_a.tile([P, 2 * DO], F32, tag="a")
-            nc.tensor.matmul(vec_ps[:], lhsT=ones[:], rhs=vec_rows[:], start=True, stop=True)
-            for r in range(2):
-                nc.vector.tensor_copy(out=m_bc[:, r, :], in_=vec_ps[:, 0:DO])
-                nc.vector.tensor_copy(out=b_bc[:, r, :], in_=vec_ps[:, DO : 2 * DO])
 
         def transposes(i):
             o_words = o_tiles[i][:].bitcast(F32)
-            go = work.tile([P, T * P * 4], BF16, align_bytes=64)
-            go_tiles[i] = go
-            go_words = go[:].bitcast(F32).rearrange("p (j r u) -> p j r u", j=T, u=2)
+            grp = work.tile([P, 2, T * P * 4], BF16, align_bytes=64)
+            grp_tiles[i] = grp
+            go_words = grp[:, 0, :].bitcast(F32).rearrange("p (j r u) -> p j r u", j=T, u=2)
             for half in range(2):
                 xt = ps_a.tile([P, 2, 2, P], F32, tag="a")
                 for jj in range(2):
@@ -106,65 +110,54 @@ def tile_gatblock_pa_t_kernel(tc, h_norm, o_attn, a_gcn, w_proj, b_proj, gcn_w, 
                 )
 
         def mix(i, b):
-            if b == 0:
-                gg = work.tile([P, T, P, 4], BF16, align_bytes=64)
-                gg_tiles[i] = gg
             ag = ps_a.tile([P, 4, P], F32, tag="a")
             for t in range(4):
                 nc.tensor.matmul(
                     ag[:, t, :], lhsT=h_tiles[i][:, b, P * t : P * t + P], rhs=a_t[:], start=True, stop=True
                 )
-            nc.scalar.copy(
-                out=gg_tiles[i][:, :, 32 * b : 32 * b + 32, :], in_=ag[:].rearrange("p t (r j) -> p j r t", j=T)
-            )
+            gg = grp_tiles[i][:, 1, :].rearrange("p (j r t) -> p j r t", j=T, t=4)
+            nc.scalar.copy(out=gg[:, :, 32 * b : 32 * b + 32, :], in_=ag[:].rearrange("p t (r j) -> p j r t", j=T))
 
-        def quantise_o(i):
-            oc = work.tile([P, T * P], U32, align_bytes=64)
-            osc = work.tile([P, T * P], U8, align_bytes=64)
-            nc.vector.quantize_mx(out=oc[:].bitcast(FP8X4), scales=osc[:], in_=go_tiles[i][:])
-            oc_tiles[i] = oc
-            os_tiles[i] = osc
-
-        def quantise_g(i):
-            gc = work.tile([P, T * P], U32, align_bytes=64)
-            gsc = work.tile([P, T * P], U8, align_bytes=64)
+        def quantise(i):
+            codes = work.tile([P, 2 * T * P], U32, align_bytes=64)
+            scales = work.tile([P, 2 * T * P], U8, align_bytes=64)
             nc.vector.quantize_mx(
-                out=gc[:].bitcast(FP8X4), scales=gsc[:], in_=gg_tiles[i][:].rearrange("p j r t -> p (j r t)")
+                out=codes[:].bitcast(FP8X4), scales=scales[:], in_=grp_tiles[i][:].rearrange("p w c -> p (w c)")
             )
-            gc_tiles[i] = gc
-            gs_tiles[i] = gsc
+            code_tiles[i] = codes
+            scale_tiles[i] = scales
 
-        def mx_passes(i):
-            for which, codes, scales, keep in (
-                (1, gc_tiles[i], gs_tiles[i], mg_tiles),
-                (0, oc_tiles[i], os_tiles[i], mo_tiles),
-            ):
-                for half in range(2):
-                    acc = ps_m.tile([P, 2, DO], F32, tag="m%d%d" % (which, half))
-                    keep[(i, half)] = acc
-                    for jj in range(2):
-                        c0 = P * (2 * half + jj)
-                        nc.tensor.matmul_mx(
-                            out=acc[:, jj, :],
-                            lhsT=codes[:, c0 : c0 + P].bitcast(FP8X4),
-                            lhsT_scale=scales[:, c0 : c0 + P],
-                            rhs=w_codes[:, DO * which : DO * which + DO].bitcast(FP8X4),
-                            rhs_scale=w_scales[:, DO * which : DO * which + DO],
-                            start=True,
-                            stop=True,
-                        )
+        def mx_passes(i, which, half):
+            acc = ps_m.tile([P, 2, DO], F32, tag="m%d%d" % (which, half))
+            acc_tiles[(i, which, half)] = acc
+            for jj in range(2):
+                c0 = T * P * which + P * (2 * half + jj)
+                nc.tensor.matmul_mx(
+                    out=acc[:, jj, :],
+                    lhsT=code_tiles[i][:, c0 : c0 + P].bitcast(FP8X4),
+                    lhsT_scale=scale_tiles[i][:, c0 : c0 + P],
+                    rhs=w_codes[:, DO * which : DO * which + DO].bitcast(FP8X4),
+                    rhs_scale=w_scales[:, DO * which : DO * which + DO],
+                    start=True,
+                    stop=True,
+                )
 
         def scale_g(i, half):
             if half == 0:
                 res = outs.tile([P, T, DO], F32)
                 res_tiles[i] = res
             part = res_tiles[i][:, 2 * half : 2 * half + 2, :]
-            nc.vector.tensor_tensor(out=part, in0=mg_tiles[(i, half)][:], in1=m_bc[:], op=MULT)
+            nc.vector.tensor_tensor(out=part, in0=acc_tiles[(i, 1, half)][:], in1=m_bc[:], op=MULT)
 
         def add_o(i, half):
             part = res_tiles[i][:, 2 * half : 2 * half + 2, :]
-            nc.vector.tensor_tensor(out=part, in0=mo_tiles[(i, half)][:], in1=part, op=ADD)
+            nc.vector.tensor_tensor(out=part, in0=acc_tiles[(i, 0, half)][:], in1=part, op=ADD)
             nc.gpsimd.tensor_tensor(out=part, in0=part, in1=b_bc[:], op=ADD)
+            if i == NBLK - 1:
+                c0 = 2 * half * DO
+                nc.sync.dma_start(
+                    out=out_blk[i][:, c0 : c0 + 2 * DO], in_=part.rearrange("p j c -> p (j c)")
+                )
 
         def store(i):
             nc.sync.dma_start(out=out_blk[i], in_=res_tiles[i][:].rearrange("p j c -> p (j c)"))
@@ -172,27 +165,36 @@ def tile_gatblock_pa_t_kernel(tc, h_norm, o_attn, a_gcn, w_proj, b_proj, gcn_w, 
         def live(i):
             return 0 <= i < NBLK
 
-        for i in range(-2, NBLK + 1):
-            if i == 0:
-                spread_vectors()
-            if live(i):
-                quantise_g(i)
-            if live(i - 1):
-                add_o(i - 1, 1)
-                store(i - 1)
-            if live(i):
-                mx_passes(i)
-            if live(i + 1):
-                mix(i + 1, 2)
-                mix(i + 1, 3)
-                quantise_o(i + 1)
-            if live(i):
-                scale_g(i, 0)
-                scale_g(i, 1)
-                add_o(i, 0)
-            if live(i + 2):
-                transposes(i + 2)
-                mix(i + 2, 0)
-                mix(i + 2, 1)
-            if live(i + 2 + LEAD):
-                load(i + 2 + LEAD)
+        for w in range(-AHEAD - 1, NBLK + 2):
+            f = w + AHEAD
+            if live(w + 1):
+                quantise(w + 1)
+            if live(w - 2) and w - 2 < NBLK - 1:
+                store(w - 2)
+            if live(w - 1):
+                mx_passes(w - 1, 0, 1)
+            if live(f - 1):
+                mix(f - 1, 3)
+            if live(f):
+                transposes(f)
+                mix(f, 0)
+            if live(w - 1):
+                add_o(w - 1, 0)
+            if live(w):
+                mx_passes(w, 0, 0)
+            if live(f):
+                mix(f, 1)
+            if live(w):
+                scale_g(w, 0)
+            if live(w + 1):
+                mx_passes(w + 1, 1, 0)
+            if live(f):
+                mix(f, 2)
+            if live(w):
+                scale_g(w, 1)
+            if live(w + 1):
+                mx_passes(w + 1, 1, 1)
+            if live(w - 1):
+                add_o(w - 1, 1)
+            if live(f + 1 + LEAD):
+                load(f + 1 + LEAD, 1)

@@ -16,7 +16,7 @@ B, N, D, DO = 64, 128, 512, 256
 T = 4
 NBLK = B // T
 LEAD = 8
-AHEAD = 3
+VECTOR_COPIES = ((0, 1), (0, 3), (0, 5), (1, 4))
 FLOPS = 2 * 2 * B * N * D * DO + 2 * B * N * N * D
 
 
@@ -28,7 +28,7 @@ def tile_gatblock_pa_t_kernel(tc, h_norm, o_attn, a_gcn, w_proj, b_proj, gcn_w, 
 
     with ExitStack() as ctx:
         consts = ctx.enter_context(tc.tile_pool(name="consts", bufs=1))
-        inputs = ctx.enter_context(tc.tile_pool(name="inputs", bufs=LEAD + 3))
+        inputs = ctx.enter_context(tc.tile_pool(name="inputs", bufs=LEAD + 2))
         work = ctx.enter_context(tc.tile_pool(name="work", bufs=3))
         outs = ctx.enter_context(tc.tile_pool(name="outs", bufs=8))
         ps_a = ctx.enter_context(tc.psum_pool(name="ps_a", bufs=4))
@@ -82,8 +82,8 @@ def tile_gatblock_pa_t_kernel(tc, h_norm, o_attn, a_gcn, w_proj, b_proj, gcn_w, 
         vec_ps = ps_a.tile([P, 2 * DO], F32, tag="a")
         nc.tensor.matmul(vec_ps[:], lhsT=ones[:], rhs=vec_rows[:], start=True, stop=True)
         for r in range(2):
-            nc.vector.tensor_copy(out=m_bc[:, r, :], in_=vec_ps[:, 0:DO])
-            nc.vector.tensor_copy(out=b_bc[:, r, :], in_=vec_ps[:, DO : 2 * DO])
+            nc.scalar.copy(out=m_bc[:, r, :], in_=vec_ps[:, 0:DO])
+            nc.scalar.copy(out=b_bc[:, r, :], in_=vec_ps[:, DO : 2 * DO])
 
         w_grp = consts.tile([P, 2, DO, 4], BF16, align_bytes=64)
         w_codes = consts.tile([P, 2 * DO], U32, align_bytes=64)
@@ -93,6 +93,12 @@ def tile_gatblock_pa_t_kernel(tc, h_norm, o_attn, a_gcn, w_proj, b_proj, gcn_w, 
         nc.vector.quantize_mx(
             out=w_codes[:].bitcast(FP8X4), scales=w_scales[:], in_=w_grp[:].rearrange("p w c t -> p (w c t)")
         )
+
+        def copy_out(i, bank, dst, src):
+            if (i, bank) in VECTOR_COPIES:
+                nc.vector.tensor_copy(out=dst, in_=src)
+            else:
+                nc.scalar.copy(out=dst, in_=src)
 
         def transposes(i):
             o_words = o_tiles[i][:].bitcast(F32)
@@ -105,9 +111,7 @@ def tile_gatblock_pa_t_kernel(tc, h_norm, o_attn, a_gcn, w_proj, b_proj, gcn_w, 
                     for u in range(2):
                         c0 = 256 * (2 * half + jj) + P * u
                         nc.tensor.transpose(xt[:, jj, u, :], o_words[:, c0 : c0 + P], ident[:])
-                nc.scalar.copy(
-                    out=go_words[:, 2 * half : 2 * half + 2, :, :], in_=xt[:].rearrange("p j u r -> p j r u")
-                )
+                copy_out(i, half, go_words[:, 2 * half : 2 * half + 2, :, :], xt[:].rearrange("p j u r -> p j r u"))
 
         def mix(i, b):
             ag = ps_a.tile([P, 4, P], F32, tag="a")
@@ -116,7 +120,7 @@ def tile_gatblock_pa_t_kernel(tc, h_norm, o_attn, a_gcn, w_proj, b_proj, gcn_w, 
                     ag[:, t, :], lhsT=h_tiles[i][:, b, P * t : P * t + P], rhs=a_t[:], start=True, stop=True
                 )
             gg = grp_tiles[i][:, 1, :].rearrange("p (j r t) -> p j r t", j=T, t=4)
-            nc.scalar.copy(out=gg[:, :, 32 * b : 32 * b + 32, :], in_=ag[:].rearrange("p t (r j) -> p j r t", j=T))
+            copy_out(i, 2 + b, gg[:, :, 32 * b : 32 * b + 32, :], ag[:].rearrange("p t (r j) -> p j r t", j=T))
 
         def quantise(i):
             codes = work.tile([P, 2 * T * P], U32, align_bytes=64)
@@ -152,7 +156,10 @@ def tile_gatblock_pa_t_kernel(tc, h_norm, o_attn, a_gcn, w_proj, b_proj, gcn_w, 
         def add_o(i, half):
             part = res_tiles[i][:, 2 * half : 2 * half + 2, :]
             nc.vector.tensor_tensor(out=part, in0=acc_tiles[(i, 0, half)][:], in1=part, op=ADD)
-            nc.gpsimd.tensor_tensor(out=part, in0=part, in1=b_bc[:], op=ADD)
+            if i == NBLK - 1 and half == 1:
+                nc.vector.tensor_tensor(out=part, in0=part, in1=b_bc[:], op=ADD)
+            else:
+                nc.gpsimd.tensor_tensor(out=part, in0=part, in1=b_bc[:], op=ADD)
             if i == NBLK - 1:
                 c0 = 2 * half * DO
                 nc.sync.dma_start(
@@ -165,36 +172,34 @@ def tile_gatblock_pa_t_kernel(tc, h_norm, o_attn, a_gcn, w_proj, b_proj, gcn_w, 
         def live(i):
             return 0 <= i < NBLK
 
-        for w in range(-AHEAD - 1, NBLK + 2):
-            f = w + AHEAD
-            if live(w + 1):
-                quantise(w + 1)
+        for w in range(-2, NBLK + 1):
+            if live(w):
+                quantise(w)
             if live(w - 2) and w - 2 < NBLK - 1:
                 store(w - 2)
-            if live(w - 1):
-                mx_passes(w - 1, 0, 1)
-            if live(f - 1):
-                mix(f - 1, 3)
-            if live(f):
-                transposes(f)
-                mix(f, 0)
+            if live(w + 1):
+                mix(w + 1, 2)
+            if live(w):
+                mx_passes(w, 1, 0)
+            if live(w + 1):
+                mix(w + 1, 3)
+            if live(w + 2):
+                transposes(w + 2)
+                mix(w + 2, 0)
             if live(w - 1):
                 add_o(w - 1, 0)
             if live(w):
                 mx_passes(w, 0, 0)
-            if live(f):
-                mix(f, 1)
+            if live(w - 1):
+                scale_g(w - 1, 1)
             if live(w):
+                mx_passes(w, 1, 1)
                 scale_g(w, 0)
-            if live(w + 1):
-                mx_passes(w + 1, 1, 0)
-            if live(f):
-                mix(f, 2)
-            if live(w):
-                scale_g(w, 1)
-            if live(w + 1):
-                mx_passes(w + 1, 1, 1)
             if live(w - 1):
                 add_o(w - 1, 1)
-            if live(f + 1 + LEAD):
-                load(f + 1 + LEAD, 1)
+            if live(w):
+                mx_passes(w, 0, 1)
+            if live(w + 2):
+                mix(w + 2, 1)
+            if live(w + 2 + LEAD):
+                load(w + 2 + LEAD, 1)

@@ -17,6 +17,8 @@ T = 4
 NBLK = B // T
 LEAD = 8
 VECTOR_COPIES = ((0, 1), (0, 3), (0, 5), (1, 4))
+SPLIT_LOADS = 3
+VECTOR_BIAS = 2
 FLOPS = 2 * 2 * B * N * D * DO + 2 * B * N * N * D
 
 
@@ -62,9 +64,8 @@ def tile_gatblock_pa_t_kernel(tc, h_norm, o_attn, a_gcn, w_proj, b_proj, gcn_w, 
             out=w_raw[:, 0, :, :].rearrange("p (u e) c -> p u (e c)", u=2),
             in_=w_proj.rearrange("(u p e) c -> p u (e c)", u=2, e=2),
         )
-        load(0, 2)
-        for k in range(1, LEAD):
-            load(k, 1)
+        for k in range(LEAD):
+            load(k, 2 if k < SPLIT_LOADS else 1)
 
         ident = consts.tile([P, P], F32)
         masks.make_identity(nc, ident[:])
@@ -78,11 +79,12 @@ def tile_gatblock_pa_t_kernel(tc, h_norm, o_attn, a_gcn, w_proj, b_proj, gcn_w, 
         nc.vector.tensor_copy(out=a_t[:], in_=at_ps[:])
 
         m_bc = consts.tile([P, 2, DO], F32)
-        b_bc = consts.tile([P, 2, DO], F32)
+        b_bc = consts.tile([P, T, DO], F32)
         vec_ps = ps_a.tile([P, 2 * DO], F32, tag="a")
         nc.tensor.matmul(vec_ps[:], lhsT=ones[:], rhs=vec_rows[:], start=True, stop=True)
         for r in range(2):
             nc.scalar.copy(out=m_bc[:, r, :], in_=vec_ps[:, 0:DO])
+        for r in range(T):
             nc.scalar.copy(out=b_bc[:, r, :], in_=vec_ps[:, DO : 2 * DO])
 
         w_grp = consts.tile([P, 2, DO, 4], BF16, align_bytes=64)
@@ -156,18 +158,21 @@ def tile_gatblock_pa_t_kernel(tc, h_norm, o_attn, a_gcn, w_proj, b_proj, gcn_w, 
         def add_o(i, half):
             part = res_tiles[i][:, 2 * half : 2 * half + 2, :]
             nc.vector.tensor_tensor(out=part, in0=acc_tiles[(i, 0, half)][:], in1=part, op=ADD)
-            if i == NBLK - 1 and half == 1:
-                nc.vector.tensor_tensor(out=part, in0=part, in1=b_bc[:], op=ADD)
-            else:
-                nc.gpsimd.tensor_tensor(out=part, in0=part, in1=b_bc[:], op=ADD)
-            if i == NBLK - 1:
-                c0 = 2 * half * DO
-                nc.sync.dma_start(
-                    out=out_blk[i][:, c0 : c0 + 2 * DO], in_=part.rearrange("p j c -> p (j c)")
-                )
+
+        def bias_block(i):
+            nc.gpsimd.tensor_tensor(out=res_tiles[i][:], in0=res_tiles[i][:], in1=b_bc[:], op=ADD)
 
         def store(i):
             nc.sync.dma_start(out=out_blk[i], in_=res_tiles[i][:].rearrange("p j c -> p (j c)"))
+
+        def bias_and_store_half(i, half):
+            part = res_tiles[i][:, 2 * half : 2 * half + 2, :]
+            nc.vector.tensor_tensor(out=part, in0=part, in1=b_bc[:, 0:2, :], op=ADD)
+            c0 = 2 * half * DO
+            nc.sync.dma_start(out=out_blk[i][:, c0 : c0 + 2 * DO], in_=part.rearrange("p j c -> p (j c)"))
+
+        def late(i):
+            return NBLK - VECTOR_BIAS <= i < NBLK
 
         def live(i):
             return 0 <= i < NBLK
@@ -175,7 +180,7 @@ def tile_gatblock_pa_t_kernel(tc, h_norm, o_attn, a_gcn, w_proj, b_proj, gcn_w, 
         for w in range(-2, NBLK + 1):
             if live(w):
                 quantise(w)
-            if live(w - 2) and w - 2 < NBLK - 1:
+            if live(w - 2) and not late(w - 2):
                 store(w - 2)
             if live(w + 1):
                 mix(w + 1, 2)
@@ -188,18 +193,25 @@ def tile_gatblock_pa_t_kernel(tc, h_norm, o_attn, a_gcn, w_proj, b_proj, gcn_w, 
                 mix(w + 2, 0)
             if live(w - 1):
                 add_o(w - 1, 0)
+            if late(w - 2):
+                bias_and_store_half(w - 2, 1)
             if live(w):
                 mx_passes(w, 0, 0)
             if live(w - 1):
                 scale_g(w - 1, 1)
+            if late(w - 1):
+                bias_and_store_half(w - 1, 0)
             if live(w):
                 mx_passes(w, 1, 1)
                 scale_g(w, 0)
             if live(w - 1):
                 add_o(w - 1, 1)
+                if not late(w - 1):
+                    bias_block(w - 1)
             if live(w):
                 mx_passes(w, 0, 1)
             if live(w + 2):
                 mix(w + 2, 1)
             if live(w + 2 + LEAD):
                 load(w + 2 + LEAD, 1)
+        bias_and_store_half(NBLK - 1, 1)

@@ -17,8 +17,6 @@ T = 4
 NBLK = B // T
 LEAD = 8
 VECTOR_COPIES = ((0, 1), (0, 3), (0, 5), (1, 4))
-SPLIT_LOADS = 3
-VECTOR_BIAS = 2
 FLOPS = 2 * 2 * B * N * D * DO + 2 * B * N * N * D
 
 
@@ -32,7 +30,7 @@ def tile_gatblock_pa_t_kernel(tc, h_norm, o_attn, a_gcn, w_proj, b_proj, gcn_w, 
         consts = ctx.enter_context(tc.tile_pool(name="consts", bufs=1))
         inputs = ctx.enter_context(tc.tile_pool(name="inputs", bufs=LEAD + 2))
         work = ctx.enter_context(tc.tile_pool(name="work", bufs=3))
-        outs = ctx.enter_context(tc.tile_pool(name="outs", bufs=8))
+        outs = ctx.enter_context(tc.tile_pool(name="outs", bufs=12))
         ps_a = ctx.enter_context(tc.psum_pool(name="ps_a", bufs=4))
         ps_m = ctx.enter_context(tc.psum_pool(name="ps_m", bufs=1))
         ctx.enter_context(tc.manual_schedule())
@@ -64,8 +62,9 @@ def tile_gatblock_pa_t_kernel(tc, h_norm, o_attn, a_gcn, w_proj, b_proj, gcn_w, 
             out=w_raw[:, 0, :, :].rearrange("p (u e) c -> p u (e c)", u=2),
             in_=w_proj.rearrange("(u p e) c -> p u (e c)", u=2, e=2),
         )
-        for k in range(LEAD):
-            load(k, 2 if k < SPLIT_LOADS else 1)
+        load(0, 2)
+        for k in range(1, LEAD):
+            load(k, 1)
 
         ident = consts.tile([P, P], F32)
         masks.make_identity(nc, ident[:])
@@ -79,12 +78,11 @@ def tile_gatblock_pa_t_kernel(tc, h_norm, o_attn, a_gcn, w_proj, b_proj, gcn_w, 
         nc.vector.tensor_copy(out=a_t[:], in_=at_ps[:])
 
         m_bc = consts.tile([P, 2, DO], F32)
-        b_bc = consts.tile([P, T, DO], F32)
+        b_bc = consts.tile([P, 2, DO], F32)
         vec_ps = ps_a.tile([P, 2 * DO], F32, tag="a")
         nc.tensor.matmul(vec_ps[:], lhsT=ones[:], rhs=vec_rows[:], start=True, stop=True)
         for r in range(2):
             nc.scalar.copy(out=m_bc[:, r, :], in_=vec_ps[:, 0:DO])
-        for r in range(T):
             nc.scalar.copy(out=b_bc[:, r, :], in_=vec_ps[:, DO : 2 * DO])
 
         w_grp = consts.tile([P, 2, DO, 4], BF16, align_bytes=64)
@@ -158,21 +156,18 @@ def tile_gatblock_pa_t_kernel(tc, h_norm, o_attn, a_gcn, w_proj, b_proj, gcn_w, 
         def add_o(i, half):
             part = res_tiles[i][:, 2 * half : 2 * half + 2, :]
             nc.vector.tensor_tensor(out=part, in0=acc_tiles[(i, 0, half)][:], in1=part, op=ADD)
-
-        def bias_block(i):
-            nc.gpsimd.tensor_tensor(out=res_tiles[i][:], in0=res_tiles[i][:], in1=b_bc[:], op=ADD)
+            if i == NBLK - 1 and half == 1:
+                nc.vector.tensor_tensor(out=part, in0=part, in1=b_bc[:], op=ADD)
+            else:
+                nc.gpsimd.tensor_tensor(out=part, in0=part, in1=b_bc[:], op=ADD)
+            if i == NBLK - 1:
+                c0 = 2 * half * DO
+                nc.sync.dma_start(
+                    out=out_blk[i][:, c0 : c0 + 2 * DO], in_=part.rearrange("p j c -> p (j c)")
+                )
 
         def store(i):
             nc.sync.dma_start(out=out_blk[i], in_=res_tiles[i][:].rearrange("p j c -> p (j c)"))
-
-        def bias_and_store_half(i, half):
-            part = res_tiles[i][:, 2 * half : 2 * half + 2, :]
-            nc.vector.tensor_tensor(out=part, in0=part, in1=b_bc[:, 0:2, :], op=ADD)
-            c0 = 2 * half * DO
-            nc.sync.dma_start(out=out_blk[i][:, c0 : c0 + 2 * DO], in_=part.rearrange("p j c -> p (j c)"))
-
-        def late(i):
-            return NBLK - VECTOR_BIAS <= i < NBLK
 
         def live(i):
             return 0 <= i < NBLK
@@ -180,7 +175,7 @@ def tile_gatblock_pa_t_kernel(tc, h_norm, o_attn, a_gcn, w_proj, b_proj, gcn_w, 
         for w in range(-2, NBLK + 1):
             if live(w):
                 quantise(w)
-            if live(w - 2) and not late(w - 2):
+            if live(w - 2) and w - 2 < NBLK - 1:
                 store(w - 2)
             if live(w + 1):
                 mix(w + 1, 2)
@@ -193,25 +188,18 @@ def tile_gatblock_pa_t_kernel(tc, h_norm, o_attn, a_gcn, w_proj, b_proj, gcn_w, 
                 mix(w + 2, 0)
             if live(w - 1):
                 add_o(w - 1, 0)
-            if late(w - 2):
-                bias_and_store_half(w - 2, 1)
             if live(w):
                 mx_passes(w, 0, 0)
             if live(w - 1):
                 scale_g(w - 1, 1)
-            if late(w - 1):
-                bias_and_store_half(w - 1, 0)
             if live(w):
                 mx_passes(w, 1, 1)
                 scale_g(w, 0)
             if live(w - 1):
                 add_o(w - 1, 1)
-                if not late(w - 1):
-                    bias_block(w - 1)
             if live(w):
                 mx_passes(w, 0, 1)
             if live(w + 2):
                 mix(w + 2, 1)
             if live(w + 2 + LEAD):
                 load(w + 2 + LEAD, 1)
-        bias_and_store_half(NBLK - 1, 1)

from contextlib import ExitStack

import concourse.masks as masks
import concourse.mybir as mybir

F32 = mybir.dt.float32
BF16 = mybir.dt.bfloat16
U32 = mybir.dt.uint32
U8 = mybir.dt.uint8
FP8X4 = mybir.dt.float8_e4m3fn_x4
MULT = mybir.AluOpType.mult
ADD = mybir.AluOpType.add

P = 128
B, N, D, DO = 64, 128, 512, 256
T = 4
NBLK = B // T
LEAD = 8
VECTOR_COPIES = ((0, 1), (0, 3), (0, 5), (1, 4))
FLOPS = 2 * 2 * B * N * D * DO + 2 * B * N * N * D


def tile_gatblock_pa_t_kernel(tc, h_norm, o_attn, a_gcn, w_proj, b_proj, gcn_w, gcn_m, out):
    nc = tc.nc
    o_blk = o_attn.flatten_outer_dims().rearrange("(k p j) d -> k p (j d)", p=P, j=T)
    out_blk = out.flatten_outer_dims().rearrange("(k p j) c -> k p (j c)", p=P, j=T)
    h_blk = h_norm.rearrange("(k b) n d -> k n b d", b=T)

    with ExitStack() as ctx:
        consts = ctx.enter_context(tc.tile_pool(name="consts", bufs=1))
        inputs = ctx.enter_context(tc.tile_pool(name="inputs", bufs=LEAD + 2))
        work = ctx.enter_context(tc.tile_pool(name="work", bufs=3))
        outs = ctx.enter_context(tc.tile_pool(name="outs", bufs=12))
        ps_a = ctx.enter_context(tc.psum_pool(name="ps_a", bufs=4))
        ps_m = ctx.enter_context(tc.psum_pool(name="ps_m", bufs=1))
        ctx.enter_context(tc.manual_schedule())

        o_tiles, h_tiles, grp_tiles, code_tiles, scale_tiles = {}, {}, {}, {}, {}
        acc_tiles, res_tiles = {}, {}

        def load(k, pieces):
            o_sb = inputs.tile([P, T * D], BF16)
            h_sb = inputs.tile([P, T, D], BF16)
            o_tiles[k] = o_sb
            h_tiles[k] = h_sb
            wo = T * D // pieces
            for q in range(pieces):
                nc.sync.dma_start(out=o_sb[:, q * wo : (q + 1) * wo], in_=o_blk[k][:, q * wo : (q + 1) * wo])
            wh = T // pieces
            for q in range(pieces):
                nc.sync.dma_start(out=h_sb[:, q * wh : (q + 1) * wh, :], in_=h_blk[k][:, q * wh : (q + 1) * wh, :])

        a_sb = consts.tile([P, P], BF16)
        nc.sync.dma_start(out=a_sb[:], in_=a_gcn)
        vec_rows = consts.tile([P, 2 * DO], BF16)
        nc.vector.memset(vec_rows[:], 0.0)
        nc.sync.dma_start(out=vec_rows[0:1, 0:DO], in_=gcn_m.rearrange("(o c) -> o c", o=1))
        nc.sync.dma_start(out=vec_rows[0:1, DO : 2 * DO], in_=b_proj.rearrange("(o c) -> o c", o=1))
        w_raw = consts.tile([P, 2, 4, DO], BF16)
        nc.sync.dma_start(out=w_raw[:, 1, :, :], in_=gcn_w.rearrange("(t p) c -> p t c", p=P))
        nc.sync.dma_start(
            out=w_raw[:, 0, :, :].rearrange("p (u e) c -> p u (e c)", u=2),
            in_=w_proj.rearrange("(u p e) c -> p u (e c)", u=2, e=2),
        )
        load(0, 2)
        for k in range(1, LEAD):
            load(k, 1)

        ident = consts.tile([P, P], F32)
        masks.make_identity(nc, ident[:])
        ones = consts.tile([P, P], BF16)
        nc.vector.memset(ones[:], 1.0)
        ident_bf = consts.tile([P, P], BF16)
        nc.vector.tensor_copy(out=ident_bf[:], in_=ident[:])
        at_ps = ps_a.tile([P, P], BF16, tag="a")
        nc.tensor.transpose(at_ps[:], a_sb[:], ident_bf[:])
        a_t = consts.tile([P, P], BF16)
        nc.vector.tensor_copy(out=a_t[:], in_=at_ps[:])

        m_bc = consts.tile([P, 2, DO], F32)
        b_bc = consts.tile([P, 2, DO], F32)
        vec_ps = ps_a.tile([P, 2 * DO], F32, tag="a")
        nc.tensor.matmul(vec_ps[:], lhsT=ones[:], rhs=vec_rows[:], start=True, stop=True)
        for r in range(2):
            nc.scalar.copy(out=m_bc[:, r, :], in_=vec_ps[:, 0:DO])
            nc.scalar.copy(out=b_bc[:, r, :], in_=vec_ps[:, DO : 2 * DO])

        w_grp = consts.tile([P, 2, DO, 4], BF16, align_bytes=64)
        w_codes = consts.tile([P, 2 * DO], U32, align_bytes=64)
        w_scales = consts.tile([P, 2 * DO], U8, align_bytes=64)
        for w in (1, 0):
            nc.vector.tensor_copy(out=w_grp[:, w, :, :], in_=w_raw[:, w, :, :].rearrange("p t c -> p c t"))
        nc.vector.quantize_mx(
            out=w_codes[:].bitcast(FP8X4), scales=w_scales[:], in_=w_grp[:].rearrange("p w c t -> p (w c t)")
        )

        def copy_out(i, bank, dst, src):
            if (i, bank) in VECTOR_COPIES:
                nc.vector.tensor_copy(out=dst, in_=src)
            else:
                nc.scalar.copy(out=dst, in_=src)

        def transposes(i):
            o_words = o_tiles[i][:].bitcast(F32)
            grp = work.tile([P, 2, T * P * 4], BF16, align_bytes=64)
            grp_tiles[i] = grp
            go_words = grp[:, 0, :].bitcast(F32).rearrange("p (j r u) -> p j r u", j=T, u=2)
            for half in range(2):
                xt = ps_a.tile([P, 2, 2, P], F32, tag="a")
                for jj in range(2):
                    for u in range(2):
                        c0 = 256 * (2 * half + jj) + P * u
                        nc.tensor.transpose(xt[:, jj, u, :], o_words[:, c0 : c0 + P], ident[:])
                copy_out(i, half, go_words[:, 2 * half : 2 * half + 2, :, :], xt[:].rearrange("p j u r -> p j r u"))

        def mix(i, b):
            ag = ps_a.tile([P, 4, P], F32, tag="a")
            for t in range(4):
                nc.tensor.matmul(
                    ag[:, t, :], lhsT=h_tiles[i][:, b, P * t : P * t + P], rhs=a_t[:], start=True, stop=True
                )
            gg = grp_tiles[i][:, 1, :].rearrange("p (j r t) -> p j r t", j=T, t=4)
            copy_out(i, 2 + b, gg[:, :, 32 * b : 32 * b + 32, :], ag[:].rearrange("p t (r j) -> p j r t", j=T))

        def quantise(i):
            codes = work.tile([P, 2 * T * P], U32, align_bytes=64)
            scales = work.tile([P, 2 * T * P], U8, align_bytes=64)
            nc.vector.quantize_mx(
                out=codes[:].bitcast(FP8X4), scales=scales[:], in_=grp_tiles[i][:].rearrange("p w c -> p (w c)")
            )
            code_tiles[i] = codes
            scale_tiles[i] = scales

        def mx_passes(i, which, half):
            acc = ps_m.tile([P, 2, DO], F32, tag="m%d%d" % (which, half))
            acc_tiles[(i, which, half)] = acc
            for jj in range(2):
                c0 = T * P * which + P * (2 * half + jj)
                nc.tensor.matmul_mx(
                    out=acc[:, jj, :],
                    lhsT=code_tiles[i][:, c0 : c0 + P].bitcast(FP8X4),
                    lhsT_scale=scale_tiles[i][:, c0 : c0 + P],
                    rhs=w_codes[:, DO * which : DO * which + DO].bitcast(FP8X4),
                    rhs_scale=w_scales[:, DO * which : DO * which + DO],
                    start=True,
                    stop=True,
                )

        def scale_g(i, half):
            if half == 0:
                res = outs.tile([P, T, DO], F32)
                res_tiles[i] = res
            part = res_tiles[i][:, 2 * half : 2 * half + 2, :]
            nc.vector.tensor_tensor(out=part, in0=acc_tiles[(i, 1, half)][:], in1=m_bc[:], op=MULT)

        def add_o(i, half):
            part = res_tiles[i][:, 2 * half : 2 * half + 2, :]
            nc.vector.tensor_tensor(out=part, in0=acc_tiles[(i, 0, half)][:], in1=part, op=ADD)
            if i == NBLK - 1 and half == 1:
                nc.vector.tensor_tensor(out=part, in0=part, in1=b_bc[:], op=ADD)
            else:
                nc.gpsimd.tensor_tensor(out=part, in0=part, in1=b_bc[:], op=ADD)
            if i == NBLK - 1:
                c0 = 2 * half * DO
                nc.sync.dma_start(
                    out=out_blk[i][:, c0 : c0 + 2 * DO], in_=part.rearrange("p j c -> p (j c)")
                )

        def store(i):
            nc.sync.dma_start(out=out_blk[i], in_=res_tiles[i][:].rearrange("p j c -> p (j c)"))

        def live(i):
            return 0 <= i < NBLK

        for w in range(-2, NBLK + 1):
            if live(w):
                quantise(w)
            if live(w - 2) and w - 2 < NBLK - 1:
                store(w - 2)
            if live(w + 1):
                mix(w + 1, 2)
            if live(w):
                mx_passes(w, 1, 0)
            if live(w + 1):
                mix(w + 1, 3)
            if live(w + 2):
                transposes(w + 2)
                mix(w + 2, 0)
            if live(w - 1):
                add_o(w - 1, 0)
            if live(w):
                mx_passes(w, 0, 0)
            if live(w - 1):
                scale_g(w - 1, 1)
            if live(w):
                mx_passes(w, 1, 1)
                scale_g(w, 0)
            if live(w - 1):
                add_o(w - 1, 1)
            if live(w):
                mx_passes(w, 0, 1)
            if live(w + 2):
                mix(w + 2, 1)
            if live(w + 2 + LEAD):
                load(w + 2 + LEAD, 1)
